import numpy as np
import ml_dtypes


def mxq(x, axis, fmt="e4m3"):
    dtype, down = {"e4m3": (ml_dtypes.float8_e4m3fn, 7), "e5m2": (ml_dtypes.float8_e5m2, 14)}[fmt]
    v = np.moveaxis(np.asarray(x, np.float32).astype(ml_dtypes.bfloat16).astype(np.float64), axis, -1)
    blocks = v.reshape(v.shape[:-1] + (-1, 32))
    amax = np.abs(blocks).max(-1, keepdims=True)
    byte = np.maximum(np.where(amax > 0, np.frexp(amax)[1] - 1 + 127, 0) - down, 1)
    scale = np.exp2(byte - 127.0)
    codes = (blocks / scale).astype(np.float32).astype(dtype).astype(np.float64)
    return np.moveaxis((codes * scale).reshape(v.shape), -1, axis)


WIDE = False


def mx_kscale(k):
    if not WIDE:
        return np.ones(k)
    levels = np.array([18, -18])
    if k % 512:
        return np.exp2(np.random.permutation(np.resize(levels, k // 32))).repeat(32)
    a = np.empty((k // 512, 16))
    for p in range(k // 512):
        a[p, :8] = np.random.permutation(np.resize(levels, 8))
        for g in range(8):
            far = levels[np.abs(levels - a[p, g]) >= 10]
            a[p, g + 8] = far[np.random.randint(len(far))]
    return np.exp2(a.ravel()).repeat(32)


BF16 = ml_dtypes.bfloat16


def bf(x):
    return np.asarray(x, np.float32).astype(BF16)


def f64(x):
    return np.asarray(x).astype(np.float64)


M, SP, H, FF, NH = 2560, 1536, 512, 2560, 8
EPS = 1.1920929e-07


def rms_norm(x, w):
    var = np.mean(np.square(x), axis=-1, keepdims=True)
    return x * (1.0 / np.sqrt(var + EPS)) * w


def setup_inputs():
    s = mx_kscale(M)[:, None]
    u = mx_kscale(3 * H)
    x0 = bf(np.random.standard_normal((M, H)))
    w0 = bf(np.random.standard_normal((2, H, 3 * H)) * 1.25 / np.sqrt(H))
    ln1 = bf(1.0 + 0.1 * np.random.standard_normal((2, H)))
    g = bf(np.random.standard_normal((M, 3 * H)) * np.exp2(np.random.randint(-6, 1, (M, 1))) / s * u)
    rstd = 1.0 / np.sqrt(np.mean(np.square(f64(x0)), axis=-1, keepdims=True) + EPS)
    return {"x": bf(f64(x0) * s), "W_qkv": bf(f64(w0) / u), "ln1": ln1,
            "rstd": np.asarray(rstd, np.float32), "grad_out": g}


def model_backward(x, w, ln, rstd, g):
    xhat = x * rstd
    h = xhat * ln
    dh = mxq(g, 1, "e5m2") @ mxq(w, 1, "e4m3").T
    dw = mxq(h, 0, "e4m3").T @ mxq(g, 0, "e5m2")
    dn = dh * ln
    dx = rstd * (dn - xhat * np.mean(dn * xhat, axis=-1, keepdims=True))
    return dx, dw


def reference(x, W_qkv, ln1, rstd, grad_out):
    x, W_qkv, ln1 = f64(x), f64(W_qkv), f64(ln1)
    rstd, g = f64(rstd), f64(grad_out)
    dx0, dw0 = model_backward(x[:SP], W_qkv[0], ln1[0], rstd[:SP], g[:SP])
    dx1, dw1 = model_backward(x[SP:], W_qkv[1], ln1[1], rstd[SP:], g[SP:])
    return np.concatenate([dx0, dx1], axis=0), np.stack([dw0, dw1], axis=0)

@@ -1,0 +1,387 @@
+from contextlib import ExitStack
+
+import concourse.mybir as mybir
+from concourse.masks import make_identity
+
+TOKENS, SPLIT, HID, FEAT = 2560, 1536, 512, 1536
+FLOPS = 2 * 2 * TOKENS * HID * FEAT
+
+F32 = mybir.dt.float32
+BF16 = mybir.dt.bfloat16
+U32 = mybir.dt.uint32
+U8 = mybir.dt.uint8
+E4M3 = mybir.dt.float8_e4m3fn_x4
+E5M2 = mybir.dt.float8_e5m2_x4
+MULT = mybir.AluOpType.mult
+ADD = mybir.AluOpType.add
+
+P = 128
+PACK = 4
+PASS = P * PACK
+GROUPS = TOKENS // PASS
+GROUPS_OF = ((0, 1, 2), (3, 4))
+CHUNKS = FEAT // PASS
+STEPS = 2 * GROUPS + 2
+
+POOL_COLS = 384
+USE_POOL = True
+DW_OF_STEP = {5: (0, 0, 4), 6: (0, 4, 6), 7: (0, 6, 10), 8: (0, 10, 12), 9: (1, 0, 4)}
+
+
+def tile_twomodelblockrouted_pa_v_kernel(tc, x, W_qkv, ln1, rstd, grad_out, out_0, out_1):
+    nc = tc.nc
+
+    with ExitStack() as ctx:
+        sb = ctx.enter_context(tc.tile_pool(name="sb", bufs=1))
+        ps = ctx.enter_context(tc.psum_pool(name="ps", bufs=1))
+        ctx.enter_context(tc.manual_schedule())
+
+        def sbuf(tag, shape, dtype):
+            return sb.tile(shape, dtype, name=tag, tag=tag, align_bytes=64)
+
+        def bank(n):
+            return ps.tile([P, PASS], F32, name="bank%d" % n, tag="bank%d" % n)
+
+        def model_of(g):
+            return 0 if g < len(GROUPS_OF[0]) else 1
+
+        x_sb, g_sb, w_sb = {}, {}, {}
+        h32, h_stage, t_stage = {}, {}, {}
+        h_q, t_q, f_q, w_q = {}, {}, {}, {}
+        dh_bank, dx_sb = {}, {}
+
+        def load_x(g):
+            x_sb[g] = sbuf("x%d" % g, [P, PACK, HID], BF16)
+            rows = x[g * PASS : (g + 1) * PASS, :]
+            nc.sync.dma_start(out=x_sb[g][:], in_=rows.rearrange("(p j) c -> p j c", j=PACK))
+
+        def load_g_chunk(g, k):
+            t = sbuf("gc%d" % k, [P, PACK, PASS], BF16)
+            rows = grad_out[g * PASS : (g + 1) * PASS, k * PASS : (k + 1) * PASS]
+            nc.sync.dma_start(out=t[:], in_=rows.rearrange("(p j) f -> p j f", j=PACK))
+            g_sb[g, k] = t[:]
+
+        def load_g(g):
+            t = sbuf("g%d" % (g % 2), [P, PACK, FEAT], BF16)
+            rows = grad_out[g * PASS : (g + 1) * PASS, :]
+            nc.sync.dma_start(out=t[:], in_=rows.rearrange("(p j) f -> p j f", j=PACK))
+            for k in range(CHUNKS):
+                g_sb[g, k] = t[:, :, k * PASS : (k + 1) * PASS]
+
+        def load_w(m, k):
+            w_sb[m, k] = sbuf("w%d" % k, [P, PACK, PASS], BF16)
+            cols = W_qkv[m, :, k * PASS : (k + 1) * PASS]
+            nc.sync.dma_start(out=w_sb[m, k][:], in_=cols.rearrange("(i p) f -> p i f", p=P))
+
+        stage_count = [0]
+
+        def turn(units, banks, tag=None):
+            if tag is None:
+                tag = "fstage%d" % (stage_count[0] % 3)
+                stage_count[0] = stage_count[0] + 1
+            stage = sbuf(tag, [P, len(units) * PASS], BF16)
+            words_out = stage[:].bitcast(F32)
+            for b in range(len(units) // 2):
+                acc = bank(banks[b])
+                for n in range(2):
+                    words = units[2 * b + n].bitcast(F32)
+                    for u in range(2):
+                        col = (2 * n + u) * P
+                        nc.tensor.transpose(acc[:, col : col + P], words[:, u : 2 * P : 2], ident[:])
+                nc.scalar.copy(
+                    out=words_out[:, b * PASS : (b + 1) * PASS].rearrange("p (n r u) -> p n r u", n=2, u=2),
+                    in_=acc[:].rearrange("p (n u r) -> p n r u", n=2, u=2),
+                )
+            return stage
+
+        def quantize(tag, stage, width, fmt, pieces):
+            codes = sbuf(tag + "c", [P, width], U32)
+            scales = sbuf(tag + "s", [P, width], U8)
+            for lo, hi in pieces:
+                nc.vector.quantize_mx(
+                    out=codes[:, lo:hi].bitcast(fmt),
+                    scales=scales[:, lo:hi],
+                    in_=stage[:, PACK * lo : PACK * hi],
+                )
+            return codes, scales
+
+        fq_count = [0]
+
+        def quantize_f(g, keys, stage):
+            width = len(keys) * P
+            pieces = [(0, PASS)] if width == PASS else [(0, PASS), (PASS, width)]
+            codes, scales = quantize("fq%d" % (fq_count[0] % 3), stage, width, E5M2, pieces)
+            fq_count[0] = fq_count[0] + 1
+            for n, (j, k) in enumerate(keys):
+                f_q[g, j, k] = (codes[:, n * P : (n + 1) * P], scales[:, n * P : (n + 1) * P])
+
+        def quantize_w(m, k, stage):
+            w_q[m, k] = quantize("wq%d%d" % (m, k), stage, PASS, E4M3, [(0, PASS)])
+
+        def quantize_t(g, k):
+            t_q[g, k] = quantize("tq%d%d" % (g, k), t_stage[g, k], PASS, E5M2, [(0, PASS)])
+
+        def quantize_h(g):
+            h_q[g] = quantize("hq%d" % g, h_stage[g], PASS, E4M3, [(0, PASS)])
+
+        def interleave(copy, stage, rows, lo, hi):
+            copy(
+                out=stage[:, PACK * lo : PACK * hi].rearrange("p (c i t) -> p c t i", i=4, t=PACK),
+                in_=rows[:, :, lo:hi].rearrange("p t (c i) -> p c t i", i=4),
+            )
+
+        def open_t(g, k):
+            t_stage[g, k] = sbuf("tstage%d" % k, [P, PACK * PASS], BF16)
+
+        def interleave_pool(g, k):
+            if USE_POOL:
+                nc.gpsimd.tensor_scalar(
+                    out=t_stage[g, k][:, : PACK * POOL_COLS].rearrange("p (c t) -> p c t", t=PACK),
+                    in0=g_sb[g, k][:, :, :POOL_COLS].rearrange("p t c -> p c t"),
+                    scalar1=1.0, scalar2=0.0, op0=MULT, op1=ADD,
+                )
+
+        def interleave_dve(g, k):
+            if not USE_POOL:
+                interleave(nc.vector.tensor_copy, t_stage[g, k], g_sb[g, k], 0, POOL_COLS)
+
+        def interleave_h(g):
+            h_stage[g] = sbuf("hstage%d" % (g % 2), [P, PACK * HID], BF16)
+            interleave(nc.scalar.copy, h_stage[g], h32[g][:], 0, HID)
+
+        def make_h(g, j):
+            if j == 0:
+                h32[g] = sbuf("h32_%d" % (g % 3), [P, PACK, HID], F32)
+            m = model_of(g)
+            n = PACK * g + j
+            nc.vector.scalar_tensor_tensor(
+                out=h32[g][:, j, :], in0=x_sb[g][:, j, :], scalar=rs[:, n : n + 1],
+                in1=gain[:, m * HID : (m + 1) * HID], op0=MULT, op1=MULT,
+            )
+
+        def dh_pass(g, j, k, bank_no):
+            if k == 0:
+                dh_bank[g, j] = bank(bank_no)
+            lc, ls = f_q[g, j, k]
+            rc, rsc = w_q[model_of(g), k]
+            nc.tensor.matmul_mx(
+                out=dh_bank[g, j][:], lhsT=lc.bitcast(E5M2), lhsT_scale=ls,
+                rhs=rc[:].bitcast(E4M3), rhs_scale=rsc[:], start=(k == 0), stop=(k == CHUNKS - 1),
+            )
+
+        def dh_tile(g, j, bank_no):
+            for k in range(CHUNKS):
+                dh_pass(g, j, k, bank_no)
+
+        def read_dh(g, j):
+            half, jj = divmod(j, 2)
+            if jj == 0:
+                dx_sb[g, half] = sbuf("dx%d" % ((2 * g + half) % 3), [P, 2, HID], F32)
+            m = model_of(g)
+            n = PACK * g + j
+            nc.vector.scalar_tensor_tensor(
+                out=dx_sb[g, half][:, jj, :], in0=dh_bank[g, j][:], scalar=rs[:, n : n + 1],
+                in1=gain[:, m * HID : (m + 1) * HID], op0=MULT, op1=MULT,
+            )
+            nc.vector.scalar_tensor_tensor(
+                out=products[:], in0=dh_bank[g, j][:], scalar=rs2[:, n : n + 1],
+                in1=h32[g][:, j, :], op0=MULT, op1=MULT, accum_out=coef[:, n : n + 1],
+            )
+
+        def finish_dx(g, j):
+            half, jj = divmod(j, 2)
+            n = PACK * g + j
+            nc.vector.scalar_tensor_tensor(
+                out=dx_sb[g, half][:, jj, :], in0=x_sb[g][:, j, :], scalar=coef[:, n : n + 1],
+                in1=dx_sb[g, half][:, jj, :], op0=MULT, op1=ADD,
+            )
+
+        def store_dx(g, half, lo, hi):
+            rows = out_0[g * PASS : (g + 1) * PASS, :].rearrange("(p j) c -> p j c", j=PACK)
+            nc.sync.dma_start(out=rows[:, 2 * half + lo : 2 * half + hi, :], in_=dx_sb[g, half][:, lo:hi, :])
+
+        def dw_matmuls(m, n, bank_no):
+            k, i = divmod(n, PACK)
+            acc = bank(bank_no)
+            for g in GROUPS_OF[m]:
+                hc, hs = h_q[g]
+                gc, gs = t_q[g, k]
+                nc.tensor.matmul_mx(
+                    out=acc[:], lhsT=hc[:, i * P : (i + 1) * P].bitcast(E4M3), lhsT_scale=hs[:, i * P : (i + 1) * P],
+                    rhs=gc[:].bitcast(E5M2), rhs_scale=gs[:],
+                    start=(g == GROUPS_OF[m][0]), stop=(g == GROUPS_OF[m][-1]),
+                )
+            return acc
+
+        def dw_out(m, n, acc, copy=nc.scalar.copy):
+            k, i = divmod(n, PACK)
+            res = sbuf("dw%d" % (n % 4), [P, PASS], F32)
+            copy(out=res[:], in_=acc[:])
+            nc.sync.dma_start(out=out_1[m, i * P : (i + 1) * P, k * PASS : (k + 1) * PASS], in_=res[:])
+
+        gain_cols = sbuf("gain_cols", [P, 8], BF16)
+        nc.scalar.dma_start(out=gain_cols[:], in_=ln1.rearrange("m (q i) -> (m q) i", i=8))
+        rs = sbuf("rs", [P, GROUPS * PACK], F32)
+        nc.scalar.dma_start(
+            out=rs[:].rearrange("p (g j) -> p g j", j=PACK),
+            in_=rstd.rearrange("(g p j) o -> p g (j o)", p=P, j=PACK),
+        )
+        for k in range(CHUNKS):
+            load_g_chunk(0, k)
+            if k == 0:
+                load_x(0)
+            load_w(0, k)
+        load_x(1)
+        load_g(1)
+        load_x(2)
+
+        ident = sbuf("ident", [P, P], F32)
+        make_identity(nc, ident[:])
+        gain = sbuf("gain", [P, 2 * HID], BF16)
+        acc0 = bank(0)
+        gain_words = gain_cols[:].bitcast(F32)
+        for i in range(4):
+            nc.tensor.transpose(acc0[:, i * P : (i + 1) * P], gain_words[:, i : i + 1].to_broadcast([P, P]), ident[:])
+        nc.scalar.copy(
+            out=gain[:].bitcast(F32).rearrange("p (n i) -> p n i", i=4),
+            in_=acc0[:].rearrange("p (i n) -> p n i", i=4),
+        )
+        rs2 = sbuf("rs2", [P, GROUPS * PACK], F32)
+        coef = sbuf("coef", [P, GROUPS * PACK], F32)
+        products = sbuf("products", [P, HID], F32)
+
+        head_banks = (0, 1, 6, 7)
+        for k in range(CHUNKS):
+            f_stage = turn([g_sb[0, k][:, j, :] for j in range(PACK)], (2, 3))
+            w_stage = turn([w_sb[0, k][:, i, :] for i in range(PACK)], (4, 5))
+            if k > 0:
+                for j in range(PACK):
+                    dh_pass(0, j, k - 1, head_banks[j])
+            if k < CHUNKS - 1:
+                open_t(0, k)
+                interleave(nc.vector.tensor_copy, t_stage[0, k], g_sb[0, k], 0, PASS)
+            if k == 0:
+                nc.vector.scalar_tensor_tensor(out=rs2[:], in0=rs[:], scalar=-1.0 / HID, in1=rs[:], op0=MULT, op1=MULT)
+                for j in range(PACK):
+                    make_h(0, j)
+            if k == CHUNKS - 1:
+                quantize_t(0, 0)
+            quantize_f(0, [(j, k) for j in range(PACK)], f_stage)
+            quantize_w(0, k, w_stage)
+        for j in range(PACK):
+            dh_pass(0, j, CHUNKS - 1, head_banks[j])
+        load_w(1, 0)
+        load_w(1, 1)
+        load_g(2)
+        load_w(1, 2)
+        load_x(3)
+        load_x(4)
+        interleave_h(0)
+        for j in range(PACK):
+            make_h(1, j)
+        quantize_t(0, 1)
+
+        last = GROUPS - 1
+        pending = []
+        w_stages = {}
+        for step in range(2, STEPS - 2):
+            g, half = divmod(step, 2)
+            pg, phalf = divmod(step - 2, 2)
+            qg, qhalf = divmod(step - 1, 2)
+            if half == 0 and 2 <= g < last:
+                load_g(g + 1)
+
+            open_t(g, 1 + half)
+            interleave_pool(g, 1 + half)
+
+            for item in pending:
+                dw_out(*item)
+            pending = []
+            keys = [(j, k) for j in (2 * half, 2 * half + 1) for k in range(CHUNKS)]
+            f_stage = turn([g_sb[g, k][:, j, :] for j, k in keys], (2, 3, 4))
+
+            read_dh(pg, 2 * phalf)
+            read_dh(pg, 2 * phalf + 1)
+
+            if step == 2:
+                open_t(0, 2)
+                interleave(nc.scalar.copy, t_stage[0, 2], g_sb[0, 2], 0, PASS)
+            if half == 0:
+                interleave_h(g)
+            else:
+                interleave(nc.scalar.copy, t_stage[g, 2], g_sb[g, 2], POOL_COLS, PASS)
+            if step >= 3:
+                dh_tile(qg, 2 * qhalf, 0)
+            if 3 <= step <= 5:
+                w_stages[step - 3] = turn([w_sb[1, step - 3][:, i, :] for i in range(PACK)], (5, 6), "gc%d" % (step - 3))
+            if step >= 3:
+                dh_tile(qg, 2 * qhalf + 1, 1)
+
+            if step == STEPS - 3:
+                quantize_h(g)
+                quantize_t(g, 0)
+            finish_dx(pg, 2 * phalf)
+            if g < last:
+                make_h(g + 1, 2 * half)
+            if step == STEPS - 3:
+                quantize_t(g, 1)
+            finish_dx(pg, 2 * phalf + 1)
+            store_dx(pg, phalf, 0, 2)
+            if g < last:
+                make_h(g + 1, 2 * half + 1)
+            interleave_dve(g, 1 + half)
+            if half == 1 and g < last:
+                quantize_h(g)
+                quantize_t(g, 0)
+
+            m, lo, hi = DW_OF_STEP.get(step, (0, 0, 0))
+            accs = [(m, n, dw_matmuls(m, n, 5 + (n - lo))) for n in range(lo, min(hi, lo + 3))]
+            if accs:
+                dw_out(*accs[0])
+            if hi - lo == 4:
+                accs.append((m, hi - 1, dw_matmuls(m, hi - 1, 5)))
+            if half == 0:
+                open_t(g, 0)
+                interleave(nc.scalar.copy, t_stage[g, 0], g_sb[g, 0], 0, PASS)
+                for item in accs[1:]:
+                    dw_out(*item)
+                interleave(nc.scalar.copy, t_stage[g, 1], g_sb[g, 1], POOL_COLS, PASS)
+            else:
+                for item in accs[1:-1]:
+                    dw_out(*item)
+                pending = accs[-1:]
+
+            quantize_f(g, keys, f_stage)
+            if 4 <= step <= 6:
+                quantize_w(1, step - 4, w_stages[step - 4])
+            if step == 2:
+                quantize_h(0)
+            if half == 0:
+                quantize_t(g - 1, 2)
+            elif g < last:
+                quantize_t(g, 1)
+            else:
+                quantize_t(g, 2)
+
+        for item in pending:
+            dw_out(*item)
+        dh_tile(last, 2, 2)
+        dh_tile(last, 3, 3)
+        read_dh(last, 0)
+        read_dh(last, 1)
+        finish_dx(last, 0)
+        finish_dx(last, 1)
+        tail_banks = (6, 7, 4, 5)
+        for n in range(4, 8):
+            dw_out(1, n, dw_matmuls(1, n, tail_banks[n % 4]))
+        store_dx(last, 0, 0, 2)
+        read_dh(last, 2)
+        read_dh(last, 3)
+        finish_dx(last, 2)
+        finish_dx(last, 3)
+        for n in range(8, 10):
+            dw_out(1, n, dw_matmuls(1, n, tail_banks[n % 4]))
+        store_dx(last, 1, 0, 1)
+        store_dx(last, 1, 1, 2)
+        dw_out(1, 10, dw_matmuls(1, 10, tail_banks[10 % 4]))
+        dw_out(1, 11, dw_matmuls(1, 11, tail_banks[11 % 4]), nc.vector.tensor_copy)

@@ -24,8 +24,21 @@ CHUNKS = FEAT // PASS
 STEPS = 2 * GROUPS + 2
 
 POOL_COLS = 384
-USE_POOL = True
-DW_OF_STEP = {5: (0, 0, 4), 6: (0, 4, 6), 7: (0, 6, 10), 8: (0, 10, 12), 9: (1, 0, 4)}
+WARM_FIRST = 4
+WARM_HEAD = (2,1,2,1,1,1,0)
+WARM_STEP = 0
+H_BEFORE = ((0, 1, 2, 3), (), (4, 5), (6, 7), (), (8,9), (10,11), ())
+LAST_SPLIT = 256
+DW_TAGS = ("dw0", "dw1", "dw2", "dw3", "w0", "w1", "w2", "ws0", "ws1", "ws2")
+SPLIT_FROM = 8
+FILL = (0,0,1,1,1,1,4)
+DW_NOW = 2
+DW_OF_STEP = {4: (0, 0), 5: (0, 1), 6: (0, 2), 8: (1, 0), 9: (1, 1)}
+POOL_UNIT = {2: (1, 0), 3: (2, 0), 4: (1, 1), 5: (1, 2), 6: (3, 0), 7: (4, 0), 8: (3, 1), 9: (3, 2)}
+ACT_UNIT = {2: (1, None), 3: (2, None), 4: (2, 1), 5: (2, 2), 6: (3, None), 7: (4, None), 8: (4, 1), 9: (4, 2)}
+H_OF_STEP = {3: (3, 0), 4: (3, 2), 5: (4, 0), 6: (4, 2)}
+W_OF_STEP = {2: (0, 1), 3: (2,)}
+LOADS = {3: ((3, 0), (3, 1), (3, 2)), 4: ((4, 0),), 5: ((4, 1),), 6: ((4, 2),)}
 
 
 def tile_twomodelblockrouted_pa_v_kernel(tc, x, W_qkv, ln1, rstd, grad_out, out_0, out_1):
@@ -55,18 +68,11 @@ def tile_twomodelblockrouted_pa_v_kernel(tc, x, W_qkv, ln1, rstd, grad_out, out_
             rows = x[g * PASS : (g + 1) * PASS, :]
             nc.sync.dma_start(out=x_sb[g][:], in_=rows.rearrange("(p j) c -> p j c", j=PACK))
 
-        def load_g_chunk(g, k):
-            t = sbuf("gc%d" % k, [P, PACK, PASS], BF16)
+        def load_g(g, k):
+            t = sbuf("g%d%d" % (g % 3, k), [P, PACK, PASS], BF16)
             rows = grad_out[g * PASS : (g + 1) * PASS, k * PASS : (k + 1) * PASS]
             nc.sync.dma_start(out=t[:], in_=rows.rearrange("(p j) f -> p j f", j=PACK))
             g_sb[g, k] = t[:]
-
-        def load_g(g):
-            t = sbuf("g%d" % (g % 2), [P, PACK, FEAT], BF16)
-            rows = grad_out[g * PASS : (g + 1) * PASS, :]
-            nc.sync.dma_start(out=t[:], in_=rows.rearrange("(p j) f -> p j f", j=PACK))
-            for k in range(CHUNKS):
-                g_sb[g, k] = t[:, :, k * PASS : (k + 1) * PASS]
 
         def load_w(m, k):
             w_sb[m, k] = sbuf("w%d" % k, [P, PACK, PASS], BF16)
@@ -75,7 +81,7 @@ def tile_twomodelblockrouted_pa_v_kernel(tc, x, W_qkv, ln1, rstd, grad_out, out_
 
         stage_count = [0]
 
-        def turn(units, banks, tag=None):
+        def turn(units, banks, tag=None, warm=0):
             if tag is None:
                 tag = "fstage%d" % (stage_count[0] % 3)
                 stage_count[0] = stage_count[0] + 1
@@ -83,6 +89,8 @@ def tile_twomodelblockrouted_pa_v_kernel(tc, x, W_qkv, ln1, rstd, grad_out, out_
             words_out = stage[:].bitcast(F32)
             for b in range(len(units) // 2):
                 acc = bank(banks[b])
+                for rep in range(warm):
+                    nc.tensor.matmul(acc[:], lhsT=zeros[:, :P], rhs=zeros[:], start=True, stop=True)
                 for n in range(2):
                     words = units[2 * b + n].bitcast(F32)
                     for u in range(2):
@@ -109,8 +117,8 @@ def tile_twomodelblockrouted_pa_v_kernel(tc, x, W_qkv, ln1, rstd, grad_out, out_
 
         def quantize_f(g, keys, stage):
             width = len(keys) * P
-            pieces = [(0, PASS)] if width == PASS else [(0, PASS), (PASS, width)]
-            codes, scales = quantize("fq%d" % (fq_count[0] % 3), stage, width, E5M2, pieces)
+            pieces = [(0, width)] if width < PASS else [(0, PASS), (PASS, width)]
+            codes, scales = quantize("fq%d" % (fq_count[0] % 4), stage, width, E5M2, pieces)
             fq_count[0] = fq_count[0] + 1
             for n, (j, k) in enumerate(keys):
                 f_q[g, j, k] = (codes[:, n * P : (n + 1) * P], scales[:, n * P : (n + 1) * P])
@@ -119,7 +127,7 @@ def tile_twomodelblockrouted_pa_v_kernel(tc, x, W_qkv, ln1, rstd, grad_out, out_
             w_q[m, k] = quantize("wq%d%d" % (m, k), stage, PASS, E4M3, [(0, PASS)])
 
         def quantize_t(g, k):
-            t_q[g, k] = quantize("tq%d%d" % (g, k), t_stage[g, k], PASS, E5M2, [(0, PASS)])
+            t_q[g, k] = quantize("tq%d%d" % (g % 3, k), t_stage[g, k], PASS, E5M2, [(0, PASS)])
 
         def quantize_h(g):
             h_q[g] = quantize("hq%d" % g, h_stage[g], PASS, E4M3, [(0, PASS)])
@@ -130,23 +138,18 @@ def tile_twomodelblockrouted_pa_v_kernel(tc, x, W_qkv, ln1, rstd, grad_out, out_
                 in_=rows[:, :, lo:hi].rearrange("p t (c i) -> p c t i", i=4),
             )
 
-        def open_t(g, k):
-            t_stage[g, k] = sbuf("tstage%d" % k, [P, PACK * PASS], BF16)
+        def open_t(g, k, tag):
+            t_stage[g, k] = sbuf(tag, [P, PACK * PASS], BF16)
 
         def interleave_pool(g, k):
-            if USE_POOL:
-                nc.gpsimd.tensor_scalar(
-                    out=t_stage[g, k][:, : PACK * POOL_COLS].rearrange("p (c t) -> p c t", t=PACK),
-                    in0=g_sb[g, k][:, :, :POOL_COLS].rearrange("p t c -> p c t"),
-                    scalar1=1.0, scalar2=0.0, op0=MULT, op1=ADD,
-                )
+            nc.gpsimd.tensor_scalar(
+                out=t_stage[g, k][:, : PACK * POOL_COLS].rearrange("p (c t) -> p c t", t=PACK),
+                in0=g_sb[g, k][:, :, :POOL_COLS].rearrange("p t c -> p c t"),
+                scalar1=1.0, scalar2=0.0, op0=MULT, op1=ADD,
+            )
 
-        def interleave_dve(g, k):
-            if not USE_POOL:
-                interleave(nc.vector.tensor_copy, t_stage[g, k], g_sb[g, k], 0, POOL_COLS)
-
-        def interleave_h(g):
-            h_stage[g] = sbuf("hstage%d" % (g % 2), [P, PACK * HID], BF16)
+        def interleave_h(g, tag):
+            h_stage[g] = sbuf(tag, [P, PACK * HID], BF16)
             interleave(nc.scalar.copy, h_stage[g], h32[g][:], 0, HID)
 
         def make_h(g, j):
@@ -215,7 +218,7 @@ def tile_twomodelblockrouted_pa_v_kernel(tc, x, W_qkv, ln1, rstd, grad_out, out_
 
         def dw_out(m, n, acc, copy=nc.scalar.copy):
             k, i = divmod(n, PACK)
-            res = sbuf("dw%d" % (n % 4), [P, PASS], F32)
+            res = sbuf(DW_TAGS[(12 * m + n) % len(DW_TAGS)], [P, PASS], F32)
             copy(out=res[:], in_=acc[:])
             nc.sync.dma_start(out=out_1[m, i * P : (i + 1) * P, k * PASS : (k + 1) * PASS], in_=res[:])
 
@@ -227,18 +230,22 @@ def tile_twomodelblockrouted_pa_v_kernel(tc, x, W_qkv, ln1, rstd, grad_out, out_
             in_=rstd.rearrange("(g p j) o -> p g (j o)", p=P, j=PACK),
         )
         for k in range(CHUNKS):
-            load_g_chunk(0, k)
-            if k == 0:
-                load_x(0)
+            load_g(0, k)
+            if k < CHUNKS - 1:
+                load_x(k)
             load_w(0, k)
-        load_x(1)
-        load_g(1)
-        load_x(2)
+        load_x(CHUNKS - 1)
+        for k in range(CHUNKS):
+            load_g(1, k)
 
         ident = sbuf("ident", [P, P], F32)
         make_identity(nc, ident[:])
+        zeros = sbuf("zeros", [P, PASS], BF16)
+        nc.vector.memset(zeros[:], 0.0)
         gain = sbuf("gain", [P, 2 * HID], BF16)
         acc0 = bank(0)
+        for rep in range(WARM_FIRST):
+            nc.tensor.matmul(acc0[:], lhsT=zeros[:, :P], rhs=zeros[:], start=True, stop=True)
         gain_words = gain_cols[:].bitcast(F32)
         for i in range(4):
             nc.tensor.transpose(acc0[:, i * P : (i + 1) * P], gain_words[:, i : i + 1].to_broadcast([P, P]), ident[:])
@@ -250,119 +257,143 @@ def tile_twomodelblockrouted_pa_v_kernel(tc, x, W_qkv, ln1, rstd, grad_out, out_
         coef = sbuf("coef", [P, GROUPS * PACK], F32)
         products = sbuf("products", [P, HID], F32)
 
-        head_banks = (0, 1, 6, 7)
+        h_stage[0] = sbuf("astage1", [P, PACK * HID], BF16)
+        todo = [(0, q) for q in range(4)] + [(1, q) for q in range(4)]
+        open_t(0, 2, "vstage")
+
+        def fill(count):
+            for which, q in todo[:count]:
+                if which == 1:
+                    interleave(nc.scalar.copy, t_stage[0, 2], g_sb[0, 2], q * P, (q + 1) * P)
+                else:
+                    interleave(nc.scalar.copy, h_stage[0], h32[0][:], q * P, (q + 1) * P)
+                todo.remove((which, q))
+
         for k in range(CHUNKS):
-            f_stage = turn([g_sb[0, k][:, j, :] for j in range(PACK)], (2, 3))
-            w_stage = turn([w_sb[0, k][:, i, :] for i in range(PACK)], (4, 5))
+            f_stage = turn([g_sb[0, k][:, j, :] for j in range(2)], (2 + (3 * k) % 6,), warm=WARM_HEAD[2 * k])
+            fill(FILL[2 * k])
+            w_stage = turn([w_sb[0, k][:, i, :] for i in range(PACK)], (3 + (3 * k) % 6, 4 + (3 * k) % 6), warm=WARM_HEAD[2 * k + 1])
+            fill(FILL[2 * k + 1])
             if k > 0:
-                for j in range(PACK):
-                    dh_pass(0, j, k - 1, head_banks[j])
-            if k < CHUNKS - 1:
-                open_t(0, k)
-                interleave(nc.vector.tensor_copy, t_stage[0, k], g_sb[0, k], 0, PASS)
+                for j in range(2):
+                    dh_pass(0, j, k - 1, j)
             if k == 0:
+                open_t(0, 0, "pstage")
+                interleave(nc.vector.tensor_copy, t_stage[0, 0], g_sb[0, 0], 0, PASS)
                 nc.vector.scalar_tensor_tensor(out=rs2[:], in0=rs[:], scalar=-1.0 / HID, in1=rs[:], op0=MULT, op1=MULT)
-                for j in range(PACK):
-                    make_h(0, j)
-            if k == CHUNKS - 1:
-                quantize_t(0, 0)
-            quantize_f(0, [(j, k) for j in range(PACK)], f_stage)
+            for n in H_BEFORE[2 * k]:
+                make_h(*divmod(n, PACK))
+            quantize_f(0, [(j, k) for j in range(2)], f_stage)
+            if k == 0:
+                open_t(0, 1, "astage0")
+                interleave(nc.vector.tensor_copy, t_stage[0, 1], g_sb[0, 1], 0, PASS)
+            if k == 1:
+                quantize_t(0, 1)
+            for n in H_BEFORE[2 * k + 1]:
+                make_h(*divmod(n, PACK))
             quantize_w(0, k, w_stage)
-        for j in range(PACK):
-            dh_pass(0, j, CHUNKS - 1, head_banks[j])
+        for n in H_BEFORE[6]:
+            make_h(*divmod(n, PACK))
+        late_keys = [(j, k) for j in (2, 3) for k in range(CHUNKS)]
+        late_stage = turn([g_sb[0, k][:, j, :] for j, k in late_keys], (5, 6, 7), warm=WARM_HEAD[6])
+        for j in range(2):
+            dh_pass(0, j, CHUNKS - 1, j)
         load_w(1, 0)
+        load_g(2, 0)
         load_w(1, 1)
-        load_g(2)
-        load_w(1, 2)
         load_x(3)
+        load_w(1, 2)
+        load_g(2, 1)
+        load_g(2, 2)
         load_x(4)
-        interleave_h(0)
-        for j in range(PACK):
-            make_h(1, j)
-        quantize_t(0, 1)
+        fill(FILL[6])
+        quantize_t(0, 0)
 
         last = GROUPS - 1
         pending = []
         w_stages = {}
+        w_ready = []
         for step in range(2, STEPS - 2):
             g, half = divmod(step, 2)
             pg, phalf = divmod(step - 2, 2)
             qg, qhalf = divmod(step - 1, 2)
-            if half == 0 and 2 <= g < last:
-                load_g(g + 1)
+            for item in LOADS.get(step, ()):
+                load_g(*item)
 
-            open_t(g, 1 + half)
-            interleave_pool(g, 1 + half)
+            ug, uk = POOL_UNIT[step]
+            open_t(ug, uk, "pstage")
+            interleave_pool(ug, uk)
 
             for item in pending:
                 dw_out(*item)
             pending = []
             keys = [(j, k) for j in (2 * half, 2 * half + 1) for k in range(CHUNKS)]
-            f_stage = turn([g_sb[g, k][:, j, :] for j, k in keys], (2, 3, 4))
+            f_stage = turn([g_sb[g, k][:, j, :] for j, k in keys], (2, 3, 4), warm=WARM_STEP if step <= 3 else 0)
 
             read_dh(pg, 2 * phalf)
             read_dh(pg, 2 * phalf + 1)
+            interleave(nc.scalar.copy, t_stage[ug, uk], g_sb[ug, uk], POOL_COLS, PASS)
 
             if step == 2:
-                open_t(0, 2)
-                interleave(nc.scalar.copy, t_stage[0, 2], g_sb[0, 2], 0, PASS)
-            if half == 0:
-                interleave_h(g)
+                fill(8)
+                quantize_f(0, late_keys, late_stage)
+            ag, ak = ACT_UNIT[step]
+            tag = "astage%d" % (step % 2)
+            split = LAST_SPLIT if step >= SPLIT_FROM else 0
+            if ak is None:
+                interleave_h(ag, tag)
             else:
-                interleave(nc.scalar.copy, t_stage[g, 2], g_sb[g, 2], POOL_COLS, PASS)
-            if step >= 3:
-                dh_tile(qg, 2 * qhalf, 0)
-            if 3 <= step <= 5:
-                w_stages[step - 3] = turn([w_sb[1, step - 3][:, i, :] for i in range(PACK)], (5, 6), "gc%d" % (step - 3))
-            if step >= 3:
-                dh_tile(qg, 2 * qhalf + 1, 1)
+                open_t(ag, ak, tag)
+                interleave(nc.scalar.copy, t_stage[ag, ak], g_sb[ag, ak], split, PASS)
+            w_todo = W_OF_STEP.get(step, ())
+            dh_tile(qg, 2 * qhalf, 0)
+            for k in w_todo[:1]:
+                w_stages[k] = turn([w_sb[1, k][:, i, :] for i in range(PACK)], (5, 6), "ws%d" % k)
+            dh_tile(qg, 2 * qhalf + 1, 1)
 
-            if step == STEPS - 3:
-                quantize_h(g)
-                quantize_t(g, 0)
             finish_dx(pg, 2 * phalf)
-            if g < last:
-                make_h(g + 1, 2 * half)
-            if step == STEPS - 3:
-                quantize_t(g, 1)
-            finish_dx(pg, 2 * phalf + 1)
-            store_dx(pg, phalf, 0, 2)
-            if g < last:
-                make_h(g + 1, 2 * half + 1)
-            interleave_dve(g, 1 + half)
-            if half == 1 and g < last:
-                quantize_h(g)
-                quantize_t(g, 0)
-
-            m, lo, hi = DW_OF_STEP.get(step, (0, 0, 0))
-            accs = [(m, n, dw_matmuls(m, n, 5 + (n - lo))) for n in range(lo, min(hi, lo + 3))]
-            if accs:
-                dw_out(*accs[0])
-            if hi - lo == 4:
-                accs.append((m, hi - 1, dw_matmuls(m, hi - 1, 5)))
-            if half == 0:
-                open_t(g, 0)
-                interleave(nc.scalar.copy, t_stage[g, 0], g_sb[g, 0], 0, PASS)
-                for item in accs[1:]:
-                    dw_out(*item)
-                interleave(nc.scalar.copy, t_stage[g, 1], g_sb[g, 1], POOL_COLS, PASS)
-            else:
-                for item in accs[1:-1]:
-                    dw_out(*item)
-                pending = accs[-1:]
-
-            quantize_f(g, keys, f_stage)
-            if 4 <= step <= 6:
-                quantize_w(1, step - 4, w_stages[step - 4])
             if step == 2:
                 quantize_h(0)
-            if half == 0:
-                quantize_t(g - 1, 2)
-            elif g < last:
-                quantize_t(g, 1)
             else:
-                quantize_t(g, 2)
+                vg, vk = ACT_UNIT[step - 1]
+                if vk is None:
+                    quantize_h(vg)
+                else:
+                    quantize_t(vg, vk)
+            finish_dx(pg, 2 * phalf + 1)
+            store_dx(pg, phalf, 0, 2)
 
+            if split:
+                interleave(nc.vector.tensor_copy, t_stage[ag, ak], g_sb[ag, ak], 0, split)
+            for k in w_todo[1:]:
+                w_stages[k] = turn([w_sb[1, k][:, i, :] for i in range(PACK)], (7, 5), "ws%d" % k)
+
+            if step == 2:
+                for n in H_BEFORE[7]:
+                    make_h(*divmod(n, PACK))
+            if step in H_OF_STEP:
+                hg, hj = H_OF_STEP[step]
+                make_h(hg, hj)
+                make_h(hg, hj + 1)
+
+            if step in DW_OF_STEP:
+                m, k = DW_OF_STEP[step]
+                accs = [(m, PACK * k + i, dw_matmuls(m, PACK * k + i, 5 + i)) for i in range(3)]
+                dw_out(*accs[0])
+                accs.append((m, PACK * k + 3, dw_matmuls(m, PACK * k + 3, 5)))
+                for item in accs[1:DW_NOW]:
+                    dw_out(*item)
+                pending = accs[DW_NOW:]
+
+            quantize_f(g, keys, f_stage)
+            for k in w_ready:
+                quantize_w(1, k, w_stages[k])
+            w_ready = list(w_todo)
+            if step == 3:
+                quantize_t(0, 2)
+            quantize_t(ug, uk)
+
+        quantize_t(last, 2)
         for item in pending:
             dw_out(*item)
         dh_tile(last, 2, 2)
@@ -371,17 +402,13 @@ def tile_twomodelblockrouted_pa_v_kernel(tc, x, W_qkv, ln1, rstd, grad_out, out_
         read_dh(last, 1)
         finish_dx(last, 0)
         finish_dx(last, 1)
-        tail_banks = (6, 7, 4, 5)
-        for n in range(4, 8):
-            dw_out(1, n, dw_matmuls(1, n, tail_banks[n % 4]))
-        store_dx(last, 0, 0, 2)
+        for i in range(PACK):
+            if i == 2:
+                store_dx(last, 0, 0, 2)
+            dw_out(1, 8 + i, dw_matmuls(1, 8 + i, 4 + i))
         read_dh(last, 2)
         read_dh(last, 3)
         finish_dx(last, 2)
-        finish_dx(last, 3)
-        for n in range(8, 10):
-            dw_out(1, n, dw_matmuls(1, n, tail_banks[n % 4]))
         store_dx(last, 1, 0, 1)
+        finish_dx(last, 3)
         store_dx(last, 1, 1, 2)
-        dw_out(1, 10, dw_matmuls(1, 10, tail_banks[10 % 4]))
-        dw_out(1, 11, dw_matmuls(1, 11, tail_banks[11 % 4]), nc.vector.tensor_copy)

@@ -3,7 +3,7 @@ from contextlib import ExitStack
 import concourse.mybir as mybir
 from concourse.masks import make_identity
 
-TOKENS, SPLIT, HID, FEAT = 2560, 1536, 512, 1536
+TOKENS, HID, FEAT = 2560, 512, 1536
 FLOPS = 2 * 2 * TOKENS * HID * FEAT
 
 F32 = mybir.dt.float32
@@ -19,26 +19,29 @@ P = 128
 PACK = 4
 PASS = P * PACK
 GROUPS = TOKENS // PASS
-GROUPS_OF = ((0, 1, 2), (3, 4))
 CHUNKS = FEAT // PASS
-STEPS = 2 * GROUPS + 2
+PAIRS = 2 * GROUPS
+GROUPS_OF = ((0, 1, 2), (3, 4))
+LAST_GROUP = GROUPS - 1
 
 POOL_COLS = 384
-WARM_FIRST = 4
-WARM_HEAD = (2,1,2,1,1,1,0)
-WARM_STEP = 0
-H_BEFORE = ((0, 1, 2, 3), (), (4, 5), (6, 7), (), (8,9), (10,11), ())
-LAST_SPLIT = 256
-DW_TAGS = ("dw0", "dw1", "dw2", "dw3", "w0", "w1", "w2", "ws0", "ws1", "ws2")
-SPLIT_FROM = 8
-FILL = (0,0,1,1,1,1,4)
-DW_NOW = 2
-DW_OF_STEP = {4: (0, 0), 5: (0, 1), 6: (0, 2), 8: (1, 0), 9: (1, 1)}
-POOL_UNIT = {2: (1, 0), 3: (2, 0), 4: (1, 1), 5: (1, 2), 6: (3, 0), 7: (4, 0), 8: (3, 1), 9: (3, 2)}
-ACT_UNIT = {2: (1, None), 3: (2, None), 4: (2, 1), 5: (2, 2), 6: (3, None), 7: (4, None), 8: (4, 1), 9: (4, 2)}
-H_OF_STEP = {3: (3, 0), 4: (3, 2), 5: (4, 0), 6: (4, 2)}
-W_OF_STEP = {2: (0, 1), 3: (2,)}
-LOADS = {3: ((3, 0), (3, 1), (3, 2)), 4: ((4, 0),), 5: ((4, 1),), 6: ((4, 2),)}
+DVE_COLS = 256
+
+DH_BANKS = (0, 1)
+TURN_BANKS = (2, 3, 4)
+DW_BANKS = (5, 6, 7)
+
+DW_PLACES = ("dw0", "dw1", "dw2", "dw3", "w0", "w1", "w2", "wturned0", "wturned1", "wturned2")
+
+
+def model_of(g):
+    return 0 if g in GROUPS_OF[0] else 1
+
+
+def token_work(step):
+    m, phase = divmod(step - 2, 4)
+    a, b = GROUPS_OF[m][-2:]
+    return (((a, 0), (a, None)), ((b, 0), (b, None)), ((a, 1), (b, 1)), ((a, 2), (b, 2)))[phase]
 
 
 def tile_twomodelblockrouted_pa_v_kernel(tc, x, W_qkv, ln1, rstd, grad_out, out_0, out_1):
@@ -55,44 +58,40 @@ def tile_twomodelblockrouted_pa_v_kernel(tc, x, W_qkv, ln1, rstd, grad_out, out_
         def bank(n):
             return ps.tile([P, PASS], F32, name="bank%d" % n, tag="bank%d" % n)
 
-        def model_of(g):
-            return 0 if g < len(GROUPS_OF[0]) else 1
-
         x_sb, g_sb, w_sb = {}, {}, {}
-        h32, h_stage, t_stage = {}, {}, {}
-        h_q, t_q, f_q, w_q = {}, {}, {}, {}
-        dh_bank, dx_sb = {}, {}
+        h32 = {}
+        woven = {}
+        token_q = {}
+        grad_q, w_q = {}, {}
+        dh_psum, dx_sb = {}, {}
 
         def load_x(g):
             x_sb[g] = sbuf("x%d" % g, [P, PACK, HID], BF16)
             rows = x[g * PASS : (g + 1) * PASS, :]
             nc.sync.dma_start(out=x_sb[g][:], in_=rows.rearrange("(p j) c -> p j c", j=PACK))
 
-        def load_g(g, k):
-            t = sbuf("g%d%d" % (g % 3, k), [P, PACK, PASS], BF16)
+        def load_grad(g, k):
+            g_sb[g, k] = sbuf("g%d%d" % (g % 3, k), [P, PACK, PASS], BF16)
             rows = grad_out[g * PASS : (g + 1) * PASS, k * PASS : (k + 1) * PASS]
-            nc.sync.dma_start(out=t[:], in_=rows.rearrange("(p j) f -> p j f", j=PACK))
-            g_sb[g, k] = t[:]
+            nc.sync.dma_start(out=g_sb[g, k][:], in_=rows.rearrange("(p j) f -> p j f", j=PACK))
 
         def load_w(m, k):
             w_sb[m, k] = sbuf("w%d" % k, [P, PACK, PASS], BF16)
             cols = W_qkv[m, :, k * PASS : (k + 1) * PASS]
             nc.sync.dma_start(out=w_sb[m, k][:], in_=cols.rearrange("(i p) f -> p i f", p=P))
 
-        stage_count = [0]
+        def store_dx(s, lo, hi):
+            g, half = divmod(s, 2)
+            rows = out_0[g * PASS : (g + 1) * PASS, :].rearrange("(p j) c -> p j c", j=PACK)
+            nc.sync.dma_start(out=rows[:, 2 * half + lo : 2 * half + hi, :], in_=dx_sb[s][:, lo:hi, :])
 
-        def turn(units, banks, tag=None, warm=0):
-            if tag is None:
-                tag = "fstage%d" % (stage_count[0] % 3)
-                stage_count[0] = stage_count[0] + 1
-            stage = sbuf(tag, [P, len(units) * PASS], BF16)
-            words_out = stage[:].bitcast(F32)
-            for b in range(len(units) // 2):
+        def turn(tag, blocks, banks):
+            turned = sbuf(tag, [P, len(blocks) * PASS], BF16)
+            words_out = turned[:].bitcast(F32)
+            for b in range(len(blocks) // 2):
                 acc = bank(banks[b])
-                for rep in range(warm):
-                    nc.tensor.matmul(acc[:], lhsT=zeros[:, :P], rhs=zeros[:], start=True, stop=True)
                 for n in range(2):
-                    words = units[2 * b + n].bitcast(F32)
+                    words = blocks[2 * b + n].bitcast(F32)
                     for u in range(2):
                         col = (2 * n + u) * P
                         nc.tensor.transpose(acc[:, col : col + P], words[:, u : 2 * P : 2], ident[:])
@@ -100,127 +99,130 @@ def tile_twomodelblockrouted_pa_v_kernel(tc, x, W_qkv, ln1, rstd, grad_out, out_
                     out=words_out[:, b * PASS : (b + 1) * PASS].rearrange("p (n r u) -> p n r u", n=2, u=2),
                     in_=acc[:].rearrange("p (n u r) -> p n r u", n=2, u=2),
                 )
-            return stage
+            return turned
 
-        def quantize(tag, stage, width, fmt, pieces):
-            codes = sbuf(tag + "c", [P, width], U32)
-            scales = sbuf(tag + "s", [P, width], U8)
-            for lo, hi in pieces:
-                nc.vector.quantize_mx(
-                    out=codes[:, lo:hi].bitcast(fmt),
-                    scales=scales[:, lo:hi],
-                    in_=stage[:, PACK * lo : PACK * hi],
-                )
+        def turn_w(m, k, tag, banks):
+            return turn(tag, [w_sb[m, k][:, i, :] for i in range(PACK)], banks)
+
+        def pair_blocks(s):
+            g, half = divmod(s, 2)
+            return [(g, j, k) for j in (2 * half, 2 * half + 1) for k in range(CHUNKS)]
+
+        def turn_grad(tag, keys, banks):
+            return turn(tag, [g_sb[g, k][:, j, :] for g, j, k in keys], banks)
+
+        def open_codes(tag, width):
+            return sbuf(tag + "c", [P, width], U32), sbuf(tag + "s", [P, width], U8)
+
+        def quantize(operand, source, fmt, lo, hi):
+            codes, scales = operand
+            nc.vector.quantize_mx(
+                out=codes[:, lo:hi].bitcast(fmt), scales=scales[:, lo:hi], in_=source[:, PACK * lo : PACK * hi]
+            )
+
+        def open_grad_codes(tag, keys):
+            codes, scales = open_codes(tag, len(keys) * P)
+            for n, key in enumerate(keys):
+                grad_q[key] = (codes[:, n * P : (n + 1) * P], scales[:, n * P : (n + 1) * P])
             return codes, scales
 
-        fq_count = [0]
+        def quantize_w(m, k, turned):
+            w_q[m, k] = open_codes("wq%d%d" % (m, k), PASS)
+            quantize(w_q[m, k], turned, E4M3, 0, PASS)
 
-        def quantize_f(g, keys, stage):
-            width = len(keys) * P
-            pieces = [(0, width)] if width < PASS else [(0, PASS), (PASS, width)]
-            codes, scales = quantize("fq%d" % (fq_count[0] % 4), stage, width, E5M2, pieces)
-            fq_count[0] = fq_count[0] + 1
-            for n, (j, k) in enumerate(keys):
-                f_q[g, j, k] = (codes[:, n * P : (n + 1) * P], scales[:, n * P : (n + 1) * P])
-
-        def quantize_w(m, k, stage):
-            w_q[m, k] = quantize("wq%d%d" % (m, k), stage, PASS, E4M3, [(0, PASS)])
-
-        def quantize_t(g, k):
-            t_q[g, k] = quantize("tq%d%d" % (g % 3, k), t_stage[g, k], PASS, E5M2, [(0, PASS)])
-
-        def quantize_h(g):
-            h_q[g] = quantize("hq%d" % g, h_stage[g], PASS, E4M3, [(0, PASS)])
-
-        def interleave(copy, stage, rows, lo, hi):
-            copy(
-                out=stage[:, PACK * lo : PACK * hi].rearrange("p (c i t) -> p c t i", i=4, t=PACK),
-                in_=rows[:, :, lo:hi].rearrange("p t (c i) -> p c t i", i=4),
+        def dh_pass(g, j, k, bank_no):
+            if k == 0:
+                dh_psum[g, j] = bank(bank_no)
+            grad_codes, grad_scales = grad_q[g, j, k]
+            w_codes, w_scales = w_q[model_of(g), k]
+            nc.tensor.matmul_mx(
+                out=dh_psum[g, j][:], lhsT=grad_codes.bitcast(E5M2), lhsT_scale=grad_scales,
+                rhs=w_codes[:].bitcast(E4M3), rhs_scale=w_scales[:], start=(k == 0), stop=(k == CHUNKS - 1),
             )
 
-        def open_t(g, k, tag):
-            t_stage[g, k] = sbuf(tag, [P, PACK * PASS], BF16)
-
-        def interleave_pool(g, k):
-            nc.gpsimd.tensor_scalar(
-                out=t_stage[g, k][:, : PACK * POOL_COLS].rearrange("p (c t) -> p c t", t=PACK),
-                in0=g_sb[g, k][:, :, :POOL_COLS].rearrange("p t c -> p c t"),
-                scalar1=1.0, scalar2=0.0, op0=MULT, op1=ADD,
-            )
-
-        def interleave_h(g, tag):
-            h_stage[g] = sbuf(tag, [P, PACK * HID], BF16)
-            interleave(nc.scalar.copy, h_stage[g], h32[g][:], 0, HID)
+        def dh_tile(s, jj, bank_no):
+            g, half = divmod(s, 2)
+            for k in range(CHUNKS):
+                dh_pass(g, 2 * half + jj, k, bank_no)
 
         def make_h(g, j):
             if j == 0:
                 h32[g] = sbuf("h32_%d" % (g % 3), [P, PACK, HID], F32)
-            m = model_of(g)
-            n = PACK * g + j
+            m, n = model_of(g), PACK * g + j
             nc.vector.scalar_tensor_tensor(
                 out=h32[g][:, j, :], in0=x_sb[g][:, j, :], scalar=rs[:, n : n + 1],
                 in1=gain[:, m * HID : (m + 1) * HID], op0=MULT, op1=MULT,
             )
 
-        def dh_pass(g, j, k, bank_no):
-            if k == 0:
-                dh_bank[g, j] = bank(bank_no)
-            lc, ls = f_q[g, j, k]
-            rc, rsc = w_q[model_of(g), k]
-            nc.tensor.matmul_mx(
-                out=dh_bank[g, j][:], lhsT=lc.bitcast(E5M2), lhsT_scale=ls,
-                rhs=rc[:].bitcast(E4M3), rhs_scale=rsc[:], start=(k == 0), stop=(k == CHUNKS - 1),
+        def open_woven(key, tag):
+            woven[key] = sbuf(tag, [P, PACK * PASS], BF16)
+
+        def weave(copy, key, lo, hi):
+            g, k = key
+            rows = h32[g] if k is None else g_sb[key]
+            copy(
+                out=woven[key][:, PACK * lo : PACK * hi].rearrange("p (c i j) -> p c j i", i=4, j=PACK),
+                in_=rows[:, :, lo:hi].rearrange("p j (c i) -> p c j i", i=4),
             )
 
-        def dh_tile(g, j, bank_no):
-            for k in range(CHUNKS):
-                dh_pass(g, j, k, bank_no)
-
-        def read_dh(g, j):
-            half, jj = divmod(j, 2)
-            if jj == 0:
-                dx_sb[g, half] = sbuf("dx%d" % ((2 * g + half) % 3), [P, 2, HID], F32)
-            m = model_of(g)
-            n = PACK * g + j
-            nc.vector.scalar_tensor_tensor(
-                out=dx_sb[g, half][:, jj, :], in0=dh_bank[g, j][:], scalar=rs[:, n : n + 1],
-                in1=gain[:, m * HID : (m + 1) * HID], op0=MULT, op1=MULT,
-            )
-            nc.vector.scalar_tensor_tensor(
-                out=products[:], in0=dh_bank[g, j][:], scalar=rs2[:, n : n + 1],
-                in1=h32[g][:, j, :], op0=MULT, op1=MULT, accum_out=coef[:, n : n + 1],
+        def weave_on_pool(key):
+            nc.gpsimd.tensor_scalar(
+                out=woven[key][:, : PACK * POOL_COLS].rearrange("p (c j) -> p c j", j=PACK),
+                in0=g_sb[key][:, :, :POOL_COLS].rearrange("p j c -> p c j"),
+                scalar1=1.0, scalar2=0.0, op0=MULT, op1=ADD,
             )
 
-        def finish_dx(g, j):
-            half, jj = divmod(j, 2)
-            n = PACK * g + j
-            nc.vector.scalar_tensor_tensor(
-                out=dx_sb[g, half][:, jj, :], in0=x_sb[g][:, j, :], scalar=coef[:, n : n + 1],
-                in1=dx_sb[g, half][:, jj, :], op0=MULT, op1=ADD,
-            )
+        def quantize_tokens(key):
+            g, k = key
+            if k is None:
+                token_q[key] = open_codes("hq%d" % g, PASS)
+            else:
+                token_q[key] = open_codes("tq%d%d" % (g % 3, k), PASS)
+            quantize(token_q[key], woven[key], E4M3 if k is None else E5M2, 0, PASS)
 
-        def store_dx(g, half, lo, hi):
-            rows = out_0[g * PASS : (g + 1) * PASS, :].rearrange("(p j) c -> p j c", j=PACK)
-            nc.sync.dma_start(out=rows[:, 2 * half + lo : 2 * half + hi, :], in_=dx_sb[g, half][:, lo:hi, :])
-
-        def dw_matmuls(m, n, bank_no):
-            k, i = divmod(n, PACK)
+        def dw_matmuls(m, k, i, bank_no):
             acc = bank(bank_no)
+            cols = slice(i * P, (i + 1) * P)
             for g in GROUPS_OF[m]:
-                hc, hs = h_q[g]
-                gc, gs = t_q[g, k]
+                h_codes, h_scales = token_q[g, None]
+                grad_codes, grad_scales = token_q[g, k]
                 nc.tensor.matmul_mx(
-                    out=acc[:], lhsT=hc[:, i * P : (i + 1) * P].bitcast(E4M3), lhsT_scale=hs[:, i * P : (i + 1) * P],
-                    rhs=gc[:].bitcast(E5M2), rhs_scale=gs[:],
+                    out=acc[:], lhsT=h_codes[:, cols].bitcast(E4M3), lhsT_scale=h_scales[:, cols],
+                    rhs=grad_codes[:].bitcast(E5M2), rhs_scale=grad_scales[:],
                     start=(g == GROUPS_OF[m][0]), stop=(g == GROUPS_OF[m][-1]),
                 )
-            return acc
+            return m, k, i, acc
 
-        def dw_out(m, n, acc, copy=nc.scalar.copy):
-            k, i = divmod(n, PACK)
-            res = sbuf(DW_TAGS[(12 * m + n) % len(DW_TAGS)], [P, PASS], F32)
-            copy(out=res[:], in_=acc[:])
-            nc.sync.dma_start(out=out_1[m, i * P : (i + 1) * P, k * PASS : (k + 1) * PASS], in_=res[:])
+        def dw_out(m, k, i, acc):
+            number = (m * CHUNKS + k) * PACK + i
+            result = sbuf(DW_PLACES[number % len(DW_PLACES)], [P, PASS], F32)
+            nc.scalar.copy(out=result[:], in_=acc[:])
+            nc.sync.dma_start(out=out_1[m, i * P : (i + 1) * P, k * PASS : (k + 1) * PASS], in_=result[:])
+
+        def read_dh(s):
+            g, half = divmod(s, 2)
+            m = model_of(g)
+            dx_sb[s] = sbuf("dx%d" % (s % 3), [P, 2, HID], F32)
+            for jj in range(2):
+                j = 2 * half + jj
+                n = PACK * g + j
+                nc.vector.scalar_tensor_tensor(
+                    out=dx_sb[s][:, jj, :], in0=dh_psum[g, j][:], scalar=rs[:, n : n + 1],
+                    in1=gain[:, m * HID : (m + 1) * HID], op0=MULT, op1=MULT,
+                )
+                nc.vector.scalar_tensor_tensor(
+                    out=products[:], in0=dh_psum[g, j][:], scalar=mean_factor[:, n : n + 1],
+                    in1=h32[g][:, j, :], op0=MULT, op1=MULT, accum_out=coef[:, n : n + 1],
+                )
+
+        def finish_dx(s, jj):
+            g, half = divmod(s, 2)
+            j = 2 * half + jj
+            n = PACK * g + j
+            nc.vector.scalar_tensor_tensor(
+                out=dx_sb[s][:, jj, :], in0=x_sb[g][:, j, :], scalar=coef[:, n : n + 1],
+                in1=dx_sb[s][:, jj, :], op0=MULT, op1=ADD,
+            )
 
         gain_cols = sbuf("gain_cols", [P, 8], BF16)
         nc.scalar.dma_start(out=gain_cols[:], in_=ln1.rearrange("m (q i) -> (m q) i", i=8))
@@ -230,185 +232,164 @@ def tile_twomodelblockrouted_pa_v_kernel(tc, x, W_qkv, ln1, rstd, grad_out, out_
             in_=rstd.rearrange("(g p j) o -> p g (j o)", p=P, j=PACK),
         )
         for k in range(CHUNKS):
-            load_g(0, k)
+            load_grad(0, k)
             if k < CHUNKS - 1:
                 load_x(k)
             load_w(0, k)
         load_x(CHUNKS - 1)
         for k in range(CHUNKS):
-            load_g(1, k)
+            load_grad(1, k)
 
         ident = sbuf("ident", [P, P], F32)
         make_identity(nc, ident[:])
-        zeros = sbuf("zeros", [P, PASS], BF16)
-        nc.vector.memset(zeros[:], 0.0)
+
         gain = sbuf("gain", [P, 2 * HID], BF16)
-        acc0 = bank(0)
-        for rep in range(WARM_FIRST):
-            nc.tensor.matmul(acc0[:], lhsT=zeros[:, :P], rhs=zeros[:], start=True, stop=True)
+        gain_psum = bank(DH_BANKS[0])
         gain_words = gain_cols[:].bitcast(F32)
         for i in range(4):
-            nc.tensor.transpose(acc0[:, i * P : (i + 1) * P], gain_words[:, i : i + 1].to_broadcast([P, P]), ident[:])
+            column = gain_words[:, i : i + 1].to_broadcast([P, P])
+            nc.tensor.transpose(gain_psum[:, i * P : (i + 1) * P], column, ident[:])
         nc.scalar.copy(
-            out=gain[:].bitcast(F32).rearrange("p (n i) -> p n i", i=4),
-            in_=acc0[:].rearrange("p (i n) -> p n i", i=4),
+            out=gain[:].bitcast(F32).rearrange("p (q i) -> p q i", i=4),
+            in_=gain_psum[:].rearrange("p (i q) -> p q i", i=4),
         )
-        rs2 = sbuf("rs2", [P, GROUPS * PACK], F32)
+        mean_factor = sbuf("mean_factor", [P, GROUPS * PACK], F32)
         coef = sbuf("coef", [P, GROUPS * PACK], F32)
         products = sbuf("products", [P, HID], F32)
 
-        h_stage[0] = sbuf("astage1", [P, PACK * HID], BF16)
-        todo = [(0, q) for q in range(4)] + [(1, q) for q in range(4)]
-        open_t(0, 2, "vstage")
-
-        def fill(count):
-            for which, q in todo[:count]:
-                if which == 1:
-                    interleave(nc.scalar.copy, t_stage[0, 2], g_sb[0, 2], q * P, (q + 1) * P)
-                else:
-                    interleave(nc.scalar.copy, h_stage[0], h32[0][:], q * P, (q + 1) * P)
-                todo.remove((which, q))
-
+        open_woven((0, None), "act_woven1")
         for k in range(CHUNKS):
-            f_stage = turn([g_sb[0, k][:, j, :] for j in range(2)], (2 + (3 * k) % 6,), warm=WARM_HEAD[2 * k])
-            fill(FILL[2 * k])
-            w_stage = turn([w_sb[0, k][:, i, :] for i in range(PACK)], (3 + (3 * k) % 6, 4 + (3 * k) % 6), warm=WARM_HEAD[2 * k + 1])
-            fill(FILL[2 * k + 1])
+            banks = (TURN_BANKS, DW_BANKS)[k % 2]
+            keys = [(0, j, k) for j in range(2)]
+            grad_turned = turn_grad("turned%d" % (2 * k % 3), keys, banks[:1])
             if k > 0:
+                weave(nc.scalar.copy, (0, None), (2 * k - 2) * P, (2 * k - 1) * P)
+            w_turned = turn_w(0, k, "turned%d" % ((2 * k + 1) % 3), banks[1:])
+            if k > 0:
+                weave(nc.scalar.copy, (0, None), (2 * k - 1) * P, 2 * k * P)
                 for j in range(2):
-                    dh_pass(0, j, k - 1, j)
+                    dh_pass(0, j, k - 1, DH_BANKS[j])
+
             if k == 0:
-                open_t(0, 0, "pstage")
-                interleave(nc.vector.tensor_copy, t_stage[0, 0], g_sb[0, 0], 0, PASS)
-                nc.vector.scalar_tensor_tensor(out=rs2[:], in0=rs[:], scalar=-1.0 / HID, in1=rs[:], op0=MULT, op1=MULT)
-            for n in H_BEFORE[2 * k]:
-                make_h(*divmod(n, PACK))
-            quantize_f(0, [(j, k) for j in range(2)], f_stage)
+                open_woven((0, 0), "pool_woven")
+                weave(nc.vector.tensor_copy, (0, 0), 0, PASS)
+                nc.vector.scalar_tensor_tensor(
+                    out=mean_factor[:], in0=rs[:], scalar=-1.0 / HID, in1=rs[:], op0=MULT, op1=MULT
+                )
             if k == 0:
-                open_t(0, 1, "astage0")
-                interleave(nc.vector.tensor_copy, t_stage[0, 1], g_sb[0, 1], 0, PASS)
-            if k == 1:
-                quantize_t(0, 1)
-            for n in H_BEFORE[2 * k + 1]:
-                make_h(*divmod(n, PACK))
-            quantize_w(0, k, w_stage)
-        for n in H_BEFORE[6]:
-            make_h(*divmod(n, PACK))
-        late_keys = [(j, k) for j in (2, 3) for k in range(CHUNKS)]
-        late_stage = turn([g_sb[0, k][:, j, :] for j, k in late_keys], (5, 6, 7), warm=WARM_HEAD[6])
+                for j in range(PACK):
+                    make_h(0, j)
+            quantize(open_grad_codes("gq%d" % k, keys), grad_turned, E5M2, 0, 2 * P)
+            if k == 0:
+                open_woven((0, 1), "act_woven0")
+                weave(nc.vector.tensor_copy, (0, 1), 0, PASS)
+            else:
+                make_h(k, 0)
+                make_h(k, 1)
+            quantize_w(0, k, w_turned)
+            if k > 0:
+                make_h(k, 2)
+                make_h(k, 3)
+
+        pair1_turned = turn_grad("turned0", pair_blocks(1), DW_BANKS)
         for j in range(2):
-            dh_pass(0, j, CHUNKS - 1, j)
+            dh_pass(0, j, CHUNKS - 1, DH_BANKS[j])
         load_w(1, 0)
-        load_g(2, 0)
+        load_grad(2, 0)
         load_w(1, 1)
         load_x(3)
         load_w(1, 2)
-        load_g(2, 1)
-        load_g(2, 2)
+        load_grad(2, 1)
+        load_grad(2, 2)
         load_x(4)
-        fill(FILL[6])
-        quantize_t(0, 0)
+        open_woven((0, 2), "head_woven")
+        weave(nc.scalar.copy, (0, 2), 0, PASS)
+        quantize_tokens((0, 0))
+        quantize_tokens((0, 1))
 
-        last = GROUPS - 1
-        pending = []
-        w_stages = {}
-        w_ready = []
-        for step in range(2, STEPS - 2):
-            g, half = divmod(step, 2)
-            pg, phalf = divmod(step - 2, 2)
-            qg, qhalf = divmod(step - 1, 2)
-            for item in LOADS.get(step, ()):
-                load_g(*item)
-
-            ug, uk = POOL_UNIT[step]
-            open_t(ug, uk, "pstage")
-            interleave_pool(ug, uk)
-
-            for item in pending:
-                dw_out(*item)
-            pending = []
-            keys = [(j, k) for j in (2 * half, 2 * half + 1) for k in range(CHUNKS)]
-            f_stage = turn([g_sb[g, k][:, j, :] for j, k in keys], (2, 3, 4), warm=WARM_STEP if step <= 3 else 0)
-
-            read_dh(pg, 2 * phalf)
-            read_dh(pg, 2 * phalf + 1)
-            interleave(nc.scalar.copy, t_stage[ug, uk], g_sb[ug, uk], POOL_COLS, PASS)
-
-            if step == 2:
-                fill(8)
-                quantize_f(0, late_keys, late_stage)
-            ag, ak = ACT_UNIT[step]
-            tag = "astage%d" % (step % 2)
-            split = LAST_SPLIT if step >= SPLIT_FROM else 0
-            if ak is None:
-                interleave_h(ag, tag)
-            else:
-                open_t(ag, ak, tag)
-                interleave(nc.scalar.copy, t_stage[ag, ak], g_sb[ag, ak], split, PASS)
-            w_todo = W_OF_STEP.get(step, ())
-            dh_tile(qg, 2 * qhalf, 0)
-            for k in w_todo[:1]:
-                w_stages[k] = turn([w_sb[1, k][:, i, :] for i in range(PACK)], (5, 6), "ws%d" % k)
-            dh_tile(qg, 2 * qhalf + 1, 1)
-
-            finish_dx(pg, 2 * phalf)
-            if step == 2:
-                quantize_h(0)
-            else:
-                vg, vk = ACT_UNIT[step - 1]
-                if vk is None:
-                    quantize_h(vg)
-                else:
-                    quantize_t(vg, vk)
-            finish_dx(pg, 2 * phalf + 1)
-            store_dx(pg, phalf, 0, 2)
-
-            if split:
-                interleave(nc.vector.tensor_copy, t_stage[ag, ak], g_sb[ag, ak], 0, split)
-            for k in w_todo[1:]:
-                w_stages[k] = turn([w_sb[1, k][:, i, :] for i in range(PACK)], (7, 5), "ws%d" % k)
-
-            if step == 2:
-                for n in H_BEFORE[7]:
-                    make_h(*divmod(n, PACK))
-            if step in H_OF_STEP:
-                hg, hj = H_OF_STEP[step]
-                make_h(hg, hj)
-                make_h(hg, hj + 1)
-
-            if step in DW_OF_STEP:
-                m, k = DW_OF_STEP[step]
-                accs = [(m, PACK * k + i, dw_matmuls(m, PACK * k + i, 5 + i)) for i in range(3)]
-                dw_out(*accs[0])
-                accs.append((m, PACK * k + 3, dw_matmuls(m, PACK * k + 3, 5)))
-                for item in accs[1:DW_NOW]:
-                    dw_out(*item)
-                pending = accs[DW_NOW:]
-
-            quantize_f(g, keys, f_stage)
-            for k in w_ready:
-                quantize_w(1, k, w_stages[k])
-            w_ready = list(w_todo)
+        waiting = []
+        w_turned_of = {}
+        for step in range(2, PAIRS):
             if step == 3:
-                quantize_t(0, 2)
-            quantize_t(ug, uk)
+                for k in range(CHUNKS):
+                    load_grad(3, k)
+            if 4 <= step < 4 + CHUNKS:
+                load_grad(4, step - 4)
 
-        quantize_t(last, 2)
-        for item in pending:
+            pool_key, act_key = token_work(step)
+            open_woven(pool_key, "pool_woven")
+            weave_on_pool(pool_key)
+
+            for item in waiting:
+                dw_out(*item)
+            waiting = []
+            keys = pair_blocks(step)
+            grad_turned = turn_grad("turned%d" % ((step - 1) % 3), keys, TURN_BANKS)
+
+            read_dh(step - 2)
+            weave(nc.scalar.copy, pool_key, POOL_COLS, PASS)
+            if step == 2:
+                pair1_codes = open_grad_codes("gq3", pair_blocks(1))
+                quantize(pair1_codes, pair1_turned, E5M2, PASS, 6 * P)
+                quantize(pair1_codes, pair1_turned, E5M2, 0, PASS)
+            dve_cols = DVE_COLS if step >= PAIRS - 2 else 0
+            open_woven(act_key, "act_woven%d" % (step % 2))
+            weave(nc.scalar.copy, act_key, dve_cols, PASS)
+
+            dh_tile(step - 1, 0, DH_BANKS[0])
+            if step in (2, 3):
+                k = 2 * (step - 2)
+                w_turned_of[k] = turn_w(1, k, "wturned%d" % k, DW_BANKS[:2])
+            dh_tile(step - 1, 1, DH_BANKS[1])
+
+            finish_dx(step - 2, 0)
+            quantize_tokens((0, None) if step == 2 else token_work(step - 1)[1])
+            finish_dx(step - 2, 1)
+            store_dx(step - 2, 0, 2)
+            if dve_cols:
+                weave(nc.vector.tensor_copy, act_key, 0, dve_cols)
+            if step == 2:
+                w_turned_of[1] = turn_w(1, 1, "wturned1", (DW_BANKS[2], DW_BANKS[0]))
+            if 3 <= step <= 6:
+                g, half = divmod(step - 3, 2)
+                make_h(3 + g, 2 * half)
+                make_h(3 + g, 2 * half + 1)
+
+            m, k = divmod(step - 4, 4)
+            if m >= 0 and k < CHUNKS:
+                tiles = [dw_matmuls(m, k, i, DW_BANKS[i]) for i in range(3)]
+                dw_out(*tiles[0])
+                tiles.append(dw_matmuls(m, k, 3, DW_BANKS[0]))
+                dw_out(*tiles[1])
+                waiting = tiles[2:]
+
+            if step == 3:
+                quantize_w(1, 0, w_turned_of[0])
+                quantize_w(1, 1, w_turned_of[1])
+                quantize_tokens((0, 2))
+            if step == 4:
+                quantize_w(1, 2, w_turned_of[2])
+            pair_codes = open_grad_codes("gq%d" % ((step + 2) % 4), keys)
+            quantize(pair_codes, grad_turned, E5M2, PASS, 6 * P)
+            quantize_tokens(pool_key)
+            quantize(pair_codes, grad_turned, E5M2, 0, PASS)
+
+        quantize_tokens((LAST_GROUP, CHUNKS - 1))
+        for item in waiting:
             dw_out(*item)
-        dh_tile(last, 2, 2)
-        dh_tile(last, 3, 3)
-        read_dh(last, 0)
-        read_dh(last, 1)
-        finish_dx(last, 0)
-        finish_dx(last, 1)
-        for i in range(PACK):
-            if i == 2:
-                store_dx(last, 0, 0, 2)
-            dw_out(1, 8 + i, dw_matmuls(1, 8 + i, 4 + i))
-        read_dh(last, 2)
-        read_dh(last, 3)
-        finish_dx(last, 2)
-        store_dx(last, 1, 0, 1)
-        finish_dx(last, 3)
-        store_dx(last, 1, 1, 2)
+        dh_tile(PAIRS - 1, 0, TURN_BANKS[0])
+        dh_tile(PAIRS - 1, 1, TURN_BANKS[1])
+        tail_banks = TURN_BANKS[2:] + DW_BANKS
+        tiles = [dw_matmuls(1, CHUNKS - 1, i, tail_banks[i]) for i in range(PACK)]
+        for item in tiles[:2]:
+            dw_out(*item)
+        read_dh(PAIRS - 2)
+        finish_dx(PAIRS - 2, 0)
+        finish_dx(PAIRS - 2, 1)
+        store_dx(PAIRS - 2, 0, 2)
+        for item in tiles[2:]:
+            dw_out(*item)
+        read_dh(PAIRS - 1)
+        for jj in range(2):
+            finish_dx(PAIRS - 1, jj)
+            store_dx(PAIRS - 1, jj, jj + 1)

@@ -24,8 +24,8 @@ PAIRS = 2 * GROUPS
 GROUPS_OF = ((0, 1, 2), (3, 4))
 LAST_GROUP = GROUPS - 1
 
-POOL_COLS = 384
-DVE_COLS = 256
+POOL_COLS = 432
+DVE_COLS = 128
 
 DH_BANKS = (0, 1)
 TURN_BANKS = (2, 3, 4)

@@ -25,7 +25,7 @@ GROUPS_OF = ((0, 1, 2), (3, 4))
 LAST_GROUP = GROUPS - 1
 
 POOL_COLS = 432
-DVE_COLS = 128
+DVE_COLS = 96
 
 DH_BANKS = (0, 1)
 TURN_BANKS = (2, 3, 4)
@@ -242,7 +242,6 @@ def tile_twomodelblockrouted_pa_v_kernel(tc, x, W_qkv, ln1, rstd, grad_out, out_
 
         ident = sbuf("ident", [P, P], F32)
         make_identity(nc, ident[:])
-
         gain = sbuf("gain", [P, 2 * HID], BF16)
         gain_psum = bank(DH_BANKS[0])
         gain_words = gain_cols[:].bitcast(F32)
@@ -262,11 +261,14 @@ def tile_twomodelblockrouted_pa_v_kernel(tc, x, W_qkv, ln1, rstd, grad_out, out_
             banks = (TURN_BANKS, DW_BANKS)[k % 2]
             keys = [(0, j, k) for j in range(2)]
             grad_turned = turn_grad("turned%d" % (2 * k % 3), keys, banks[:1])
-            if k > 0:
-                weave(nc.scalar.copy, (0, None), (2 * k - 2) * P, (2 * k - 1) * P)
+            if k == 1:
+                weave(nc.scalar.copy, (0, None), 0, 2 * P)
+            if k == 2:
+                weave(nc.scalar.copy, (0, None), 3 * P, 4 * P)
             w_turned = turn_w(0, k, "turned%d" % ((2 * k + 1) % 3), banks[1:])
+            if k == 1:
+                weave(nc.scalar.copy, (0, None), 2 * P, 3 * P)
             if k > 0:
-                weave(nc.scalar.copy, (0, None), (2 * k - 1) * P, 2 * k * P)
                 for j in range(2):
                     dh_pass(0, j, k - 1, DH_BANKS[j])
 
@@ -276,20 +278,20 @@ def tile_twomodelblockrouted_pa_v_kernel(tc, x, W_qkv, ln1, rstd, grad_out, out_
                 nc.vector.scalar_tensor_tensor(
                     out=mean_factor[:], in0=rs[:], scalar=-1.0 / HID, in1=rs[:], op0=MULT, op1=MULT
                 )
-            if k == 0:
                 for j in range(PACK):
                     make_h(0, j)
             quantize(open_grad_codes("gq%d" % k, keys), grad_turned, E5M2, 0, 2 * P)
             if k == 0:
                 open_woven((0, 1), "act_woven0")
                 weave(nc.vector.tensor_copy, (0, 1), 0, PASS)
-            else:
-                make_h(k, 0)
-                make_h(k, 1)
+            if k == 1:
+                for j in range(PACK):
+                    make_h(1, j)
+                quantize_tokens((0, 1))
+            if k == 2:
+                make_h(2, 0)
+                make_h(2, 1)
             quantize_w(0, k, w_turned)
-            if k > 0:
-                make_h(k, 2)
-                make_h(k, 3)
 
         pair1_turned = turn_grad("turned0", pair_blocks(1), DW_BANKS)
         for j in range(2):
@@ -304,8 +306,9 @@ def tile_twomodelblockrouted_pa_v_kernel(tc, x, W_qkv, ln1, rstd, grad_out, out_
         load_x(4)
         open_woven((0, 2), "head_woven")
         weave(nc.scalar.copy, (0, 2), 0, PASS)
+        make_h(2, 2)
         quantize_tokens((0, 0))
-        quantize_tokens((0, 1))
+        make_h(2, 3)
 
         waiting = []
         w_turned_of = {}

from contextlib import ExitStack

import concourse.mybir as mybir
from concourse.masks import make_identity

TOKENS, HID, FEAT = 2560, 512, 1536
FLOPS = 2 * 2 * TOKENS * HID * FEAT

F32 = mybir.dt.float32
BF16 = mybir.dt.bfloat16
U32 = mybir.dt.uint32
U8 = mybir.dt.uint8
E4M3 = mybir.dt.float8_e4m3fn_x4
E5M2 = mybir.dt.float8_e5m2_x4
MULT = mybir.AluOpType.mult
ADD = mybir.AluOpType.add

P = 128
PACK = 4
PASS = P * PACK
GROUPS = TOKENS // PASS
CHUNKS = FEAT // PASS
PAIRS = 2 * GROUPS
GROUPS_OF = ((0, 1, 2), (3, 4))
LAST_GROUP = GROUPS - 1

POOL_COLS = 432
DVE_COLS = 96

DH_BANKS = (0, 1)
TURN_BANKS = (2, 3, 4)
DW_BANKS = (5, 6, 7)

DW_PLACES = ("dw0", "dw1", "dw2", "dw3", "w0", "w1", "w2", "wturned0", "wturned1", "wturned2")


def model_of(g):
    return 0 if g in GROUPS_OF[0] else 1


def token_work(step):
    m, phase = divmod(step - 2, 4)
    a, b = GROUPS_OF[m][-2:]
    return (((a, 0), (a, None)), ((b, 0), (b, None)), ((a, 1), (b, 1)), ((a, 2), (b, 2)))[phase]


def tile_twomodelblockrouted_pa_v_kernel(tc, x, W_qkv, ln1, rstd, grad_out, out_0, out_1):
    nc = tc.nc

    with ExitStack() as ctx:
        sb = ctx.enter_context(tc.tile_pool(name="sb", bufs=1))
        ps = ctx.enter_context(tc.psum_pool(name="ps", bufs=1))
        ctx.enter_context(tc.manual_schedule())

        def sbuf(tag, shape, dtype):
            return sb.tile(shape, dtype, name=tag, tag=tag, align_bytes=64)

        def bank(n):
            return ps.tile([P, PASS], F32, name="bank%d" % n, tag="bank%d" % n)

        x_sb, g_sb, w_sb = {}, {}, {}
        h32 = {}
        woven = {}
        token_q = {}
        grad_q, w_q = {}, {}
        dh_psum, dx_sb = {}, {}

        def load_x(g):
            x_sb[g] = sbuf("x%d" % g, [P, PACK, HID], BF16)
            rows = x[g * PASS : (g + 1) * PASS, :]
            nc.sync.dma_start(out=x_sb[g][:], in_=rows.rearrange("(p j) c -> p j c", j=PACK))

        def load_grad(g, k):
            g_sb[g, k] = sbuf("g%d%d" % (g % 3, k), [P, PACK, PASS], BF16)
            rows = grad_out[g * PASS : (g + 1) * PASS, k * PASS : (k + 1) * PASS]
            nc.sync.dma_start(out=g_sb[g, k][:], in_=rows.rearrange("(p j) f -> p j f", j=PACK))

        def load_w(m, k):
            w_sb[m, k] = sbuf("w%d" % k, [P, PACK, PASS], BF16)
            cols = W_qkv[m, :, k * PASS : (k + 1) * PASS]
            nc.sync.dma_start(out=w_sb[m, k][:], in_=cols.rearrange("(i p) f -> p i f", p=P))

        def store_dx(s, lo, hi):
            g, half = divmod(s, 2)
            rows = out_0[g * PASS : (g + 1) * PASS, :].rearrange("(p j) c -> p j c", j=PACK)
            nc.sync.dma_start(out=rows[:, 2 * half + lo : 2 * half + hi, :], in_=dx_sb[s][:, lo:hi, :])

        def turn(tag, blocks, banks):
            turned = sbuf(tag, [P, len(blocks) * PASS], BF16)
            words_out = turned[:].bitcast(F32)
            for b in range(len(blocks) // 2):
                acc = bank(banks[b])
                for n in range(2):
                    words = blocks[2 * b + n].bitcast(F32)
                    for u in range(2):
                        col = (2 * n + u) * P
                        nc.tensor.transpose(acc[:, col : col + P], words[:, u : 2 * P : 2], ident[:])
                nc.scalar.copy(
                    out=words_out[:, b * PASS : (b + 1) * PASS].rearrange("p (n r u) -> p n r u", n=2, u=2),
                    in_=acc[:].rearrange("p (n u r) -> p n r u", n=2, u=2),
                )
            return turned

        def turn_w(m, k, tag, banks):
            return turn(tag, [w_sb[m, k][:, i, :] for i in range(PACK)], banks)

        def pair_blocks(s):
            g, half = divmod(s, 2)
            return [(g, j, k) for j in (2 * half, 2 * half + 1) for k in range(CHUNKS)]

        def turn_grad(tag, keys, banks):
            return turn(tag, [g_sb[g, k][:, j, :] for g, j, k in keys], banks)

        def open_codes(tag, width):
            return sbuf(tag + "c", [P, width], U32), sbuf(tag + "s", [P, width], U8)

        def quantize(operand, source, fmt, lo, hi):
            codes, scales = operand
            nc.vector.quantize_mx(
                out=codes[:, lo:hi].bitcast(fmt), scales=scales[:, lo:hi], in_=source[:, PACK * lo : PACK * hi]
            )

        def open_grad_codes(tag, keys):
            codes, scales = open_codes(tag, len(keys) * P)
            for n, key in enumerate(keys):
                grad_q[key] = (codes[:, n * P : (n + 1) * P], scales[:, n * P : (n + 1) * P])
            return codes, scales

        def quantize_w(m, k, turned):
            w_q[m, k] = open_codes("wq%d%d" % (m, k), PASS)
            quantize(w_q[m, k], turned, E4M3, 0, PASS)

        def dh_pass(g, j, k, bank_no):
            if k == 0:
                dh_psum[g, j] = bank(bank_no)
            grad_codes, grad_scales = grad_q[g, j, k]
            w_codes, w_scales = w_q[model_of(g), k]
            nc.tensor.matmul_mx(
                out=dh_psum[g, j][:], lhsT=grad_codes.bitcast(E5M2), lhsT_scale=grad_scales,
                rhs=w_codes[:].bitcast(E4M3), rhs_scale=w_scales[:], start=(k == 0), stop=(k == CHUNKS - 1),
            )

        def dh_tile(s, jj, bank_no):
            g, half = divmod(s, 2)
            for k in range(CHUNKS):
                dh_pass(g, 2 * half + jj, k, bank_no)

        def make_h(g, j):
            if j == 0:
                h32[g] = sbuf("h32_%d" % (g % 3), [P, PACK, HID], F32)
            m, n = model_of(g), PACK * g + j
            nc.vector.scalar_tensor_tensor(
                out=h32[g][:, j, :], in0=x_sb[g][:, j, :], scalar=rs[:, n : n + 1],
                in1=gain[:, m * HID : (m + 1) * HID], op0=MULT, op1=MULT,
            )

        def open_woven(key, tag):
            woven[key] = sbuf(tag, [P, PACK * PASS], BF16)

        def weave(copy, key, lo, hi):
            g, k = key
            rows = h32[g] if k is None else g_sb[key]
            copy(
                out=woven[key][:, PACK * lo : PACK * hi].rearrange("p (c i j) -> p c j i", i=4, j=PACK),
                in_=rows[:, :, lo:hi].rearrange("p j (c i) -> p c j i", i=4),
            )

        def weave_on_pool(key):
            nc.gpsimd.tensor_scalar(
                out=woven[key][:, : PACK * POOL_COLS].rearrange("p (c j) -> p c j", j=PACK),
                in0=g_sb[key][:, :, :POOL_COLS].rearrange("p j c -> p c j"),
                scalar1=1.0, scalar2=0.0, op0=MULT, op1=ADD,
            )

        def quantize_tokens(key):
            g, k = key
            if k is None:
                token_q[key] = open_codes("hq%d" % g, PASS)
            else:
                token_q[key] = open_codes("tq%d%d" % (g % 3, k), PASS)
            quantize(token_q[key], woven[key], E4M3 if k is None else E5M2, 0, PASS)

        def dw_matmuls(m, k, i, bank_no):
            acc = bank(bank_no)
            cols = slice(i * P, (i + 1) * P)
            for g in GROUPS_OF[m]:
                h_codes, h_scales = token_q[g, None]
                grad_codes, grad_scales = token_q[g, k]
                nc.tensor.matmul_mx(
                    out=acc[:], lhsT=h_codes[:, cols].bitcast(E4M3), lhsT_scale=h_scales[:, cols],
                    rhs=grad_codes[:].bitcast(E5M2), rhs_scale=grad_scales[:],
                    start=(g == GROUPS_OF[m][0]), stop=(g == GROUPS_OF[m][-1]),
                )
            return m, k, i, acc

        def dw_out(m, k, i, acc):
            number = (m * CHUNKS + k) * PACK + i
            result = sbuf(DW_PLACES[number % len(DW_PLACES)], [P, PASS], F32)
            nc.scalar.copy(out=result[:], in_=acc[:])
            nc.sync.dma_start(out=out_1[m, i * P : (i + 1) * P, k * PASS : (k + 1) * PASS], in_=result[:])

        def read_dh(s):
            g, half = divmod(s, 2)
            m = model_of(g)
            dx_sb[s] = sbuf("dx%d" % (s % 3), [P, 2, HID], F32)
            for jj in range(2):
                j = 2 * half + jj
                n = PACK * g + j
                nc.vector.scalar_tensor_tensor(
                    out=dx_sb[s][:, jj, :], in0=dh_psum[g, j][:], scalar=rs[:, n : n + 1],
                    in1=gain[:, m * HID : (m + 1) * HID], op0=MULT, op1=MULT,
                )
                nc.vector.scalar_tensor_tensor(
                    out=products[:], in0=dh_psum[g, j][:], scalar=mean_factor[:, n : n + 1],
                    in1=h32[g][:, j, :], op0=MULT, op1=MULT, accum_out=coef[:, n : n + 1],
                )

        def finish_dx(s, jj):
            g, half = divmod(s, 2)
            j = 2 * half + jj
            n = PACK * g + j
            nc.vector.scalar_tensor_tensor(
                out=dx_sb[s][:, jj, :], in0=x_sb[g][:, j, :], scalar=coef[:, n : n + 1],
                in1=dx_sb[s][:, jj, :], op0=MULT, op1=ADD,
            )

        gain_cols = sbuf("gain_cols", [P, 8], BF16)
        nc.scalar.dma_start(out=gain_cols[:], in_=ln1.rearrange("m (q i) -> (m q) i", i=8))
        rs = sbuf("rs", [P, GROUPS * PACK], F32)
        nc.scalar.dma_start(
            out=rs[:].rearrange("p (g j) -> p g j", j=PACK),
            in_=rstd.rearrange("(g p j) o -> p g (j o)", p=P, j=PACK),
        )
        for k in range(CHUNKS):
            load_grad(0, k)
            if k < CHUNKS - 1:
                load_x(k)
            load_w(0, k)
        load_x(CHUNKS - 1)
        for k in range(CHUNKS):
            load_grad(1, k)

        ident = sbuf("ident", [P, P], F32)
        make_identity(nc, ident[:])
        gain = sbuf("gain", [P, 2 * HID], BF16)
        gain_psum = bank(DH_BANKS[0])
        gain_words = gain_cols[:].bitcast(F32)
        for i in range(4):
            column = gain_words[:, i : i + 1].to_broadcast([P, P])
            nc.tensor.transpose(gain_psum[:, i * P : (i + 1) * P], column, ident[:])
        nc.scalar.copy(
            out=gain[:].bitcast(F32).rearrange("p (q i) -> p q i", i=4),
            in_=gain_psum[:].rearrange("p (i q) -> p q i", i=4),
        )
        mean_factor = sbuf("mean_factor", [P, GROUPS * PACK], F32)
        coef = sbuf("coef", [P, GROUPS * PACK], F32)
        products = sbuf("products", [P, HID], F32)

        open_woven((0, None), "act_woven1")
        for k in range(CHUNKS):
            banks = (TURN_BANKS, DW_BANKS)[k % 2]
            keys = [(0, j, k) for j in range(2)]
            grad_turned = turn_grad("turned%d" % (2 * k % 3), keys, banks[:1])
            if k == 1:
                weave(nc.scalar.copy, (0, None), 0, 2 * P)
            if k == 2:
                weave(nc.scalar.copy, (0, None), 3 * P, 4 * P)
            w_turned = turn_w(0, k, "turned%d" % ((2 * k + 1) % 3), banks[1:])
            if k == 1:
                weave(nc.scalar.copy, (0, None), 2 * P, 3 * P)
            if k > 0:
                for j in range(2):
                    dh_pass(0, j, k - 1, DH_BANKS[j])

            if k == 0:
                open_woven((0, 0), "pool_woven")
                weave(nc.vector.tensor_copy, (0, 0), 0, PASS)
                nc.vector.scalar_tensor_tensor(
                    out=mean_factor[:], in0=rs[:], scalar=-1.0 / HID, in1=rs[:], op0=MULT, op1=MULT
                )
                for j in range(PACK):
                    make_h(0, j)
            quantize(open_grad_codes("gq%d" % k, keys), grad_turned, E5M2, 0, 2 * P)
            if k == 0:
                open_woven((0, 1), "act_woven0")
                weave(nc.vector.tensor_copy, (0, 1), 0, PASS)
            if k == 1:
                for j in range(PACK):
                    make_h(1, j)
                quantize_tokens((0, 1))
            if k == 2:
                make_h(2, 0)
                make_h(2, 1)
            quantize_w(0, k, w_turned)

        pair1_turned = turn_grad("turned0", pair_blocks(1), DW_BANKS)
        for j in range(2):
            dh_pass(0, j, CHUNKS - 1, DH_BANKS[j])
        load_w(1, 0)
        load_grad(2, 0)
        load_w(1, 1)
        load_x(3)
        load_w(1, 2)
        load_grad(2, 1)
        load_grad(2, 2)
        load_x(4)
        open_woven((0, 2), "head_woven")
        weave(nc.scalar.copy, (0, 2), 0, PASS)
        make_h(2, 2)
        quantize_tokens((0, 0))
        make_h(2, 3)

        waiting = []
        w_turned_of = {}
        for step in range(2, PAIRS):
            if step == 3:
                for k in range(CHUNKS):
                    load_grad(3, k)
            if 4 <= step < 4 + CHUNKS:
                load_grad(4, step - 4)

            pool_key, act_key = token_work(step)
            open_woven(pool_key, "pool_woven")
            weave_on_pool(pool_key)

            for item in waiting:
                dw_out(*item)
            waiting = []
            keys = pair_blocks(step)
            grad_turned = turn_grad("turned%d" % ((step - 1) % 3), keys, TURN_BANKS)

            read_dh(step - 2)
            weave(nc.scalar.copy, pool_key, POOL_COLS, PASS)
            if step == 2:
                pair1_codes = open_grad_codes("gq3", pair_blocks(1))
                quantize(pair1_codes, pair1_turned, E5M2, PASS, 6 * P)
                quantize(pair1_codes, pair1_turned, E5M2, 0, PASS)
            dve_cols = DVE_COLS if step >= PAIRS - 2 else 0
            open_woven(act_key, "act_woven%d" % (step % 2))
            weave(nc.scalar.copy, act_key, dve_cols, PASS)

            dh_tile(step - 1, 0, DH_BANKS[0])
            if step in (2, 3):
                k = 2 * (step - 2)
                w_turned_of[k] = turn_w(1, k, "wturned%d" % k, DW_BANKS[:2])
            dh_tile(step - 1, 1, DH_BANKS[1])

            finish_dx(step - 2, 0)
            quantize_tokens((0, None) if step == 2 else token_work(step - 1)[1])
            finish_dx(step - 2, 1)
            store_dx(step - 2, 0, 2)
            if dve_cols:
                weave(nc.vector.tensor_copy, act_key, 0, dve_cols)
            if step == 2:
                w_turned_of[1] = turn_w(1, 1, "wturned1", (DW_BANKS[2], DW_BANKS[0]))
            if 3 <= step <= 6:
                g, half = divmod(step - 3, 2)
                make_h(3 + g, 2 * half)
                make_h(3 + g, 2 * half + 1)

            m, k = divmod(step - 4, 4)
            if m >= 0 and k < CHUNKS:
                tiles = [dw_matmuls(m, k, i, DW_BANKS[i]) for i in range(3)]
                dw_out(*tiles[0])
                tiles.append(dw_matmuls(m, k, 3, DW_BANKS[0]))
                dw_out(*tiles[1])
                waiting = tiles[2:]

            if step == 3:
                quantize_w(1, 0, w_turned_of[0])
                quantize_w(1, 1, w_turned_of[1])
                quantize_tokens((0, 2))
            if step == 4:
                quantize_w(1, 2, w_turned_of[2])
            pair_codes = open_grad_codes("gq%d" % ((step + 2) % 4), keys)
            quantize(pair_codes, grad_turned, E5M2, PASS, 6 * P)
            quantize_tokens(pool_key)
            quantize(pair_codes, grad_turned, E5M2, 0, PASS)

        quantize_tokens((LAST_GROUP, CHUNKS - 1))
        for item in waiting:
            dw_out(*item)
        dh_tile(PAIRS - 1, 0, TURN_BANKS[0])
        dh_tile(PAIRS - 1, 1, TURN_BANKS[1])
        tail_banks = TURN_BANKS[2:] + DW_BANKS
        tiles = [dw_matmuls(1, CHUNKS - 1, i, tail_banks[i]) for i in range(PACK)]
        for item in tiles[:2]:
            dw_out(*item)
        read_dh(PAIRS - 2)
        finish_dx(PAIRS - 2, 0)
        finish_dx(PAIRS - 2, 1)
        store_dx(PAIRS - 2, 0, 2)
        for item in tiles[2:]:
            dw_out(*item)
        read_dh(PAIRS - 1)
        for jj in range(2):
            finish_dx(PAIRS - 1, jj)
            store_dx(PAIRS - 1, jj, jj + 1)
